import numpy as np
import ml_dtypes


def mxq(x, axis, fmt="e4m3"):
    dtype, down = {"e4m3": (ml_dtypes.float8_e4m3fn, 7), "e5m2": (ml_dtypes.float8_e5m2, 14)}[fmt]
    v = np.moveaxis(np.asarray(x, np.float32).astype(ml_dtypes.bfloat16).astype(np.float64), axis, -1)
    blocks = v.reshape(v.shape[:-1] + (-1, 32))
    amax = np.abs(blocks).max(-1, keepdims=True)
    byte = np.maximum(np.where(amax > 0, np.frexp(amax)[1] - 1 + 127, 0) - down, 1)
    scale = np.exp2(byte - 127.0)
    codes = (blocks / scale).astype(np.float32).astype(dtype).astype(np.float64)
    return np.moveaxis((codes * scale).reshape(v.shape), -1, axis)


WIDE = False


def mx_kscale(k):
    if not WIDE:
        return np.ones(k)
    levels = np.array([10, -10, 5, -5, 0])
    a = np.random.permutation(np.resize(levels, k // 512 * 4)).reshape(k // 512, 4)
    idx = np.arange(k)
    return np.exp2(a[idx // 512, idx % 128 // 32])


BF16 = ml_dtypes.bfloat16


def bf(x):
    return np.asarray(x, np.float32).astype(BF16)


def f64(x):
    return np.asarray(x).astype(np.float64)


M, N, IN_CH, HID, N_CLS, DEG = 3072, 3072, 512, 128, 40, 24


def setup_inputs():
    s = mx_kscale(IN_CH)
    return {"x": bf(np.random.standard_normal((N, IN_CH)) * s),
            "adj": bf(np.random.uniform(size=(M, N)) < DEG / N),
            "W_in": bf(np.random.standard_normal((IN_CH, HID)) * 2.0 / np.sqrt(IN_CH) / s[:, None]),
            "b_in": bf(np.random.standard_normal(HID) * 0.3)}


def reference(x, adj, W_in, b_in):
    a = f64(adj)
    h = (mxq(f64(x), 1, "e4m3") @ mxq(f64(W_in), 0, "e4m3")) + f64(b_in)
    deg = np.sum(a, axis=1, keepdims=True)
    return (mxq(a, 1, "e4m3") @ mxq(h, 0, "e4m3")) / (deg + 1.0)

@@ -1,0 +1,332 @@
+from contextlib import ExitStack
+
+import concourse.mybir as mybir
+from concourse.masks import make_identity
+
+F32 = mybir.dt.float32
+BF16 = mybir.dt.bfloat16
+U32 = mybir.dt.uint32
+U8 = mybir.dt.uint8
+FP8X4 = mybir.dt.float8_e4m3fn_x4
+ALU = mybir.AluOpType
+ACTF = mybir.ActivationFunctionType
+AX = mybir.AxisListType
+
+P = 128
+NODES = 3072
+FEAT = 512
+HID = 128
+FLOPS = 2 * NODES * FEAT * HID + 2 * NODES * NODES * HID
+
+G = 2
+NS = NODES // (P * G)
+NPASS = NODES // 512
+ROWW = NODES // 2
+BANKS = 3 * G
+ABUFS = 5
+DEGN = 16
+ECOL = 448
+PIN = True
+MODES = ["PV"] * (NS - 1) + ["VV"]
+
+
+def tile_allgnn_pa_kernel(tc, x, adj, W_in, b_in, out):
+    nc = tc.nc
+    adj_v = adj.rearrange("(s p g) j -> s p (g j)", p=P, g=G)
+    out_v = out.rearrange("(s p g) h -> s p (g h)", p=P, g=G)
+    x_v = x.rearrange("(c u p e) k -> c p u (e k)", c=NPASS, u=2, p=P, e=2)
+    w_v = W_in.rearrange("(u p e) h -> p u (e h)", u=2, p=P, e=2)
+
+    with ExitStack() as ctx:
+        const = ctx.enter_context(tc.tile_pool(name="const", bufs=1))
+        apool = ctx.enter_context(tc.tile_pool(name="apool", bufs=ABUFS))
+        gpool = ctx.enter_context(tc.tile_pool(name="gpool", bufs=3))
+        small = ctx.enter_context(tc.tile_pool(name="small", bufs=4))
+        ps_t = ctx.enter_context(tc.psum_pool(name="ps_t", bufs=5))
+        ps_a = ctx.enter_context(tc.psum_pool(name="ps_a", bufs=2))
+        ps_d = ctx.enter_context(tc.psum_pool(name="ps_d", bufs=1))
+        if PIN:
+            ctx.enter_context(tc.manual_schedule())
+
+        w_raw = const.tile([P, 4 * HID], BF16)
+        nc.scalar.dma_start(out=w_raw[:].rearrange("p (u f) -> p u f", u=2), in_=w_v)
+        bias = const.tile([P, HID], BF16)
+        nc.scalar.dma_start(out=bias[:], in_=b_in.partition_broadcast(P))
+        x_sb = const.tile([P, NPASS * 2048], BF16)
+        for c in range(NPASS):
+            nc.sync.dma_start(
+                out=x_sb[:, c * 2048 : (c + 1) * 2048].rearrange("p (u f) -> p u f", u=2),
+                in_=x_v[c],
+            )
+        a_tiles = {}
+
+        def load_adj(s):
+            a_sb = apool.tile([P, G * NODES], BF16, name="a_sb")
+            nc.sync.dma_start(out=a_sb[:], in_=adj_v[s])
+            a_tiles[s] = a_sb
+
+        for s in range(ABUFS):
+            load_adj(s)
+
+        ident = const.tile([P, P], F32)
+        make_identity(nc, ident[:])
+        ones = const.tile([P, DEGN], BF16)
+        nc.vector.memset(ones[:], 1.0)
+        fold_q = const.tile([P, 32], F32)
+        nc.vector.tensor_reduce(
+            out=fold_q[:], in_=ident[:].rearrange("p (q t) -> p q t", t=4), axis=AX.X, op=ALU.add
+        )
+        fold = const.tile([P, 4, 32], F32)
+        nc.vector.tensor_copy(out=fold[:], in_=fold_q[:].unsqueeze(1).to_broadcast([P, 4, 32]))
+        quad = const.tile([P, 4], F32)
+        nc.vector.tensor_reduce(
+            out=quad[:], in_=ident[:].rearrange("p (r q) -> p r q", q=32), axis=AX.X, op=ALU.add
+        )
+        junk = const.tile([P, NODES], BF16)
+
+        w_grp = const.tile([P, 4 * HID], BF16, align_bytes=64)
+        nc.vector.tensor_copy(
+            out=w_grp[:].rearrange("p (h t) -> p h t", t=4),
+            in_=w_raw[:].rearrange("p (t h) -> p h t", t=4),
+        )
+        w_codes = const.tile([P, HID], U32, align_bytes=64)
+        w_scales = const.tile([P, HID], U8, align_bytes=64)
+        nc.vector.quantize_mx(out=w_codes[:].bitcast(FP8X4), scales=w_scales[:], in_=w_grp[:])
+
+        x_codes = const.tile([P, NPASS * 512], U32, align_bytes=64)
+        x_scales = const.tile([P, NPASS * 512], U8, align_bytes=64)
+        h_grp = const.tile([P, NPASS * 512], BF16, align_bytes=64)
+        h_codes = const.tile([P, NPASS * HID], U32, align_bytes=64)
+        h_scales = const.tile([P, NPASS * HID], U8, align_bytes=64)
+
+        def transpose_bank(words, offs):
+            tp = ps_t.tile([P, 2, 2, P], F32, name="tp")
+            for n in range(2):
+                for u in range(2):
+                    o = offs[n] + P * u
+                    nc.tensor.transpose(tp[:, n, u, :], words[:, o : o + P], ident[:])
+            return tp
+
+        def copy_bank(tp, dst_words):
+            nc.scalar.copy(
+                out=dst_words.rearrange("p (n i u) -> p n i u", n=2, i=P, u=2),
+                in_=tp[:].rearrange("p n u i -> p n i u"),
+            )
+
+        x_words = x_sb[:].bitcast(F32)
+        gx_tiles = {}
+
+        def stage1_transpose(c):
+            gx = gpool.tile([P, 2048], BF16, name="gx", align_bytes=64)
+            gx_tiles[c] = gx
+            gxw = gx[:].bitcast(F32)
+            for k in range(2):
+                tp = transpose_bank(x_words, [(c * 4 + 2 * k + n) * 256 for n in range(2)])
+                copy_bank(tp, gxw[:, k * 512 : (k + 1) * 512])
+
+        def stage1_quantise(c):
+            nc.vector.quantize_mx(
+                out=x_codes[:, c * 512 : (c + 1) * 512].bitcast(FP8X4),
+                scales=x_scales[:, c * 512 : (c + 1) * 512],
+                in_=gx_tiles[c][:],
+            )
+
+        def stage1_matmul(c):
+            ps1 = ps_a.tile([P, 4, HID], F32, name="acc")
+            for t in range(4):
+                cols = slice(c * 512 + t * P, c * 512 + (t + 1) * P)
+                nc.tensor.matmul_mx(
+                    out=ps1[:, t, :],
+                    lhsT=x_codes[:, cols].bitcast(FP8X4),
+                    lhsT_scale=x_scales[:, cols],
+                    rhs=w_codes[:].bitcast(FP8X4),
+                    rhs_scale=w_scales[:],
+                    start=True,
+                    stop=True,
+                )
+            hs = slice(c * 512, (c + 1) * 512)
+            nc.vector.tensor_tensor(
+                out=h_grp[:, hs].rearrange("p (h t) -> p h t", t=4),
+                in0=ps1[:].rearrange("p t h -> p h t"),
+                in1=bias[:].unsqueeze(2).to_broadcast([P, HID, 4]),
+                op=ALU.add,
+            )
+            nc.vector.quantize_mx(
+                out=h_codes[:, c * HID : (c + 1) * HID].bitcast(FP8X4),
+                scales=h_scales[:, c * HID : (c + 1) * HID],
+                in_=h_grp[:, hs],
+            )
+
+        for c in range(NPASS + 2):
+            if c < NPASS:
+                stage1_transpose(c)
+            if 0 <= c - 1 < NPASS:
+                stage1_quantise(c - 1)
+            if c - 2 >= 0:
+                stage1_matmul(c - 2)
+
+        g_tiles = {}
+        c_tiles = {}
+        s_tiles = {}
+        acc_tiles = {}
+        de_tiles = {}
+        dsb_tiles = {}
+        dp1_tiles = {}
+        rec_tiles = {}
+
+        def p_list(s):
+            return [g for g in range(G) if MODES[s][g] == "P"]
+
+        def has_p(s):
+            return 0 <= s < NS and len(p_list(s)) > 0
+
+        def vector_degrees(s):
+            dp1 = small.tile([P, G], F32, name="dp1")
+            dp1_tiles[s] = dp1
+            for g in range(G):
+                if MODES[s][g] == "V":
+                    nc.vector.tensor_scalar(
+                        out=junk[:],
+                        in0=a_tiles[s][:, g * NODES : (g + 1) * NODES],
+                        scalar1=1.0,
+                        scalar2=1.0,
+                        op0=ALU.mult,
+                        op1=ALU.add,
+                        accum_out=dp1[:, g : g + 1],
+                    )
+
+        def transposes(s):
+            grp = gpool.tile([P, G * NODES], BF16, name="grp", align_bytes=64)
+            g_tiles[s] = grp
+            gw = grp[:].bitcast(F32)
+            aw = a_tiles[s][:].bitcast(F32)
+            for k in range(BANKS):
+                g, kk = divmod(k, 3)
+                tp = transpose_bank(aw, [g * ROWW + (2 * kk + n) * 256 for n in range(2)])
+                copy_bank(tp, gw[:, g * ROWW + kk * 512 : g * ROWW + (kk + 1) * 512])
+            codes = gpool.tile([P, G * 768], U32, name="codes", align_bytes=64)
+            scales = gpool.tile([P, G * 768], U8, name="scales", align_bytes=64)
+            c_tiles[s] = codes
+            s_tiles[s] = scales
+
+        def quantise(s, k):
+            g, kk = divmod(k, 3)
+            w0 = g * 768 + kk * 256
+            nc.vector.quantize_mx(
+                out=c_tiles[s][:, w0 : w0 + 256].bitcast(FP8X4),
+                scales=s_tiles[s][:, w0 : w0 + 256],
+                in_=g_tiles[s][:, 4 * w0 : 4 * w0 + 1024],
+            )
+
+        def aggregate(s):
+            acc = ps_a.tile([P, 4, HID], F32, name="acc")
+            acc_tiles[s] = acc
+            for g in range(G):
+                for c in range(NPASS):
+                    cols = slice(g * 768 + c * P, g * 768 + (c + 1) * P)
+                    nc.tensor.matmul_mx(
+                        out=acc[:, g, :],
+                        lhsT=c_tiles[s][:, cols].bitcast(FP8X4),
+                        lhsT_scale=s_tiles[s][:, cols],
+                        rhs=h_codes[:, c * HID : (c + 1) * HID].bitcast(FP8X4),
+                        rhs_scale=h_scales[:, c * HID : (c + 1) * HID],
+                        start=(c == 0),
+                        stop=(c == NPASS - 1),
+                    )
+
+        def tensor_degrees(s):
+            de = ps_d.tile([P, 512], F32, name="de")
+            de_tiles[s] = de
+            for n, g in enumerate(p_list(s)):
+                for r in range(4):
+                    col = (n * 4 + r) * DEGN
+                    for c in range(NPASS):
+                        o = g * NODES + c * 512 + r * P
+                        nc.tensor.matmul(
+                            out=de[:, col : col + DEGN],
+                            lhsT=g_tiles[s][:, o : o + P],
+                            rhs=ones[:],
+                            start=(c == 0),
+                            stop=(c == NPASS - 1),
+                        )
+
+        def degrees_to_sbuf(s):
+            npt = len(p_list(s))
+            dsb = small.tile([P, 4 * G], F32, name="dsb")
+            dsb_tiles[s] = dsb
+            nc.vector.tensor_scalar(
+                out=dsb[:, 0 : 4 * npt].unsqueeze(2),
+                in0=de_tiles[s][:, 0 : 4 * npt * DEGN].rearrange("p (r n) -> p r n", n=DEGN)[:, :, 0:1],
+                scalar1=0.25,
+                scalar2=None,
+                op0=ALU.add,
+            )
+
+        def fold_degrees(s):
+            npt = len(p_list(s))
+            nc.tensor.matmul(
+                out=de_tiles[s][:, ECOL : ECOL + 4 * npt],
+                lhsT=fold[:].rearrange("p r q -> p (r q)"),
+                rhs=dsb_tiles[s][:, 0 : 4 * npt],
+                start=True,
+                stop=True,
+            )
+
+        def reciprocals(s):
+            pl = p_list(s)
+            npt = len(pl)
+            if npt > 0:
+                pick = small.tile([P, G, 4], F32, name="pick")
+                nc.vector.tensor_tensor(
+                    out=pick[:, 0:npt, :],
+                    in0=de_tiles[s][:, ECOL : ECOL + 4 * npt].rearrange("p (n r) -> p n r", r=4),
+                    in1=quad[:].unsqueeze(1).to_broadcast([P, npt, 4]),
+                    op=ALU.mult,
+                )
+                nc.vector.tensor_reduce(
+                    out=dp1_tiles[s][:, pl[0] : pl[0] + npt], in_=pick[:, 0:npt, :], axis=AX.X, op=ALU.add
+                )
+            rec = small.tile([P, G], F32, name="rec")
+            rec_tiles[s] = rec
+            nc.vector.reciprocal(out=rec[:], in_=dp1_tiles[s][:])
+
+        def finish(s):
+            o_sb = small.tile([P, G * HID], F32, name="o_sb")
+            for g in range(G):
+                nc.scalar.activation(
+                    out=o_sb[:, g * HID : (g + 1) * HID],
+                    in_=acc_tiles[s][:, g, :],
+                    func=ACTF.Copy,
+                    scale=rec_tiles[s][:, g : g + 1],
+                )
+            nc.sync.dma_start(out=out_v[s], in_=o_sb[:])
+
+        for tau in range(-1, NS + 1):
+            sp, s0, s1 = tau - 1, tau, tau + 1
+            if has_p(sp):
+                degrees_to_sbuf(sp)
+            if s1 < NS:
+                vector_degrees(s1)
+                transposes(s1)
+                if s1 + ABUFS < NS:
+                    load_adj(s1 + ABUFS)
+            if has_p(sp):
+                fold_degrees(sp)
+            if s1 < NS:
+                quantise(s1, 0)
+                quantise(s1, 1)
+                if not has_p(s1):
+                    reciprocals(s1)
+            if has_p(sp):
+                reciprocals(sp)
+            if s1 < NS:
+                for k in range(2, BANKS):
+                    quantise(s1, k)
+            if 0 <= s0 < NS:
+                aggregate(s0)
+                if has_p(s0):
+                    tensor_degrees(s0)
+            if has_p(sp):
+                finish(sp)
+            if 0 <= s0 < NS and not has_p(s0):
+                finish(s0)

@@ -7,6 +7,7 @@ F32 = mybir.dt.float32
 BF16 = mybir.dt.bfloat16
 U32 = mybir.dt.uint32
 U8 = mybir.dt.uint8
+I32 = mybir.dt.int32
 FP8X4 = mybir.dt.float8_e4m3fn_x4
 ALU = mybir.AluOpType
 ACTF = mybir.ActivationFunctionType
@@ -24,10 +25,12 @@ NPASS = NODES // 512
 ROWW = NODES // 2
 BANKS = 3 * G
 ABUFS = 5
-DEGN = 16
+DEGN = 28
 ECOL = 448
 PIN = True
-MODES = ["PV"] * (NS - 1) + ["VV"]
+MODES = ["PV"] * NS
+WARM = 4
+PIECES = {0: 6, 1: 3}
 
 
 def tile_allgnn_pa_kernel(tc, x, adj, W_in, b_in, out):
@@ -42,8 +45,8 @@ def tile_allgnn_pa_kernel(tc, x, adj, W_in, b_in, out):
         apool = ctx.enter_context(tc.tile_pool(name="apool", bufs=ABUFS))
         gpool = ctx.enter_context(tc.tile_pool(name="gpool", bufs=3))
         small = ctx.enter_context(tc.tile_pool(name="small", bufs=4))
-        ps_t = ctx.enter_context(tc.psum_pool(name="ps_t", bufs=5))
-        ps_a = ctx.enter_context(tc.psum_pool(name="ps_a", bufs=2))
+        ps_t = ctx.enter_context(tc.psum_pool(name="ps_t", bufs=6))
+        ps_a = ctx.enter_context(tc.psum_pool(name="ps_a", bufs=1))
         ps_d = ctx.enter_context(tc.psum_pool(name="ps_d", bufs=1))
         if PIN:
             ctx.enter_context(tc.manual_schedule())
@@ -62,12 +65,37 @@ def tile_allgnn_pa_kernel(tc, x, adj, W_in, b_in, out):
 
         def load_adj(s):
             a_sb = apool.tile([P, G * NODES], BF16, name="a_sb")
-            nc.sync.dma_start(out=a_sb[:], in_=adj_v[s])
+            n_piece = PIECES.get(s, 1)
+            width = G * NODES // n_piece
+            for i in range(n_piece):
+                nc.sync.dma_start(
+                    out=a_sb[:, i * width : (i + 1) * width], in_=adj_v[s][:, i * width : (i + 1) * width]
+                )
             a_tiles[s] = a_sb
 
         for s in range(ABUFS):
             load_adj(s)
 
+        idle_codes = const.tile([P, 512], U32, align_bytes=64)
+        idle_scales = const.tile([P, 512], U8, align_bytes=64)
+        idle_src = const.tile([P, 2048], BF16, align_bytes=64)
+        nc.vector.memset(idle_src[:].bitcast(I32), 0)
+        nc.vector.quantize_mx(out=idle_codes[:].bitcast(FP8X4), scales=idle_scales[:], in_=idle_src[:])
+
+        def idle_passes(n):
+            tp = ps_t.tile([P, 2, 2, P], F32, name="tp")
+            for i in range(n):
+                nc.tensor.matmul_mx(
+                    out=tp[:].rearrange("p a b c -> p (a b c)"),
+                    lhsT=idle_codes[:, 0:P].bitcast(FP8X4),
+                    lhsT_scale=idle_scales[:, 0:P],
+                    rhs=idle_codes[:].bitcast(FP8X4),
+                    rhs_scale=idle_scales[:],
+                    start=True,
+                    stop=True,
+                )
+
+        idle_passes(WARM)
         ident = const.tile([P, P], F32)
         make_identity(nc, ident[:])
         ones = const.tile([P, DEGN], BF16)
@@ -144,6 +172,7 @@ def tile_allgnn_pa_kernel(tc, x, adj, W_in, b_in, out):
                     start=True,
                     stop=True,
                 )
+            idle_passes(1)
             hs = slice(c * 512, (c + 1) * 512)
             nc.vector.tensor_tensor(
                 out=h_grp[:, hs].rearrange("p (h t) -> p h t", t=4),
@@ -160,6 +189,8 @@ def tile_allgnn_pa_kernel(tc, x, adj, W_in, b_in, out):
         for c in range(NPASS + 2):
             if c < NPASS:
                 stage1_transpose(c)
+                if c < 2:
+                    idle_passes(1)
             if 0 <= c - 1 < NPASS:
                 stage1_quantise(c - 1)
             if c - 2 >= 0:
@@ -195,19 +226,19 @@ def tile_allgnn_pa_kernel(tc, x, adj, W_in, b_in, out):
                         accum_out=dp1[:, g : g + 1],
                     )
 
-        def transposes(s):
-            grp = gpool.tile([P, G * NODES], BF16, name="grp", align_bytes=64)
-            g_tiles[s] = grp
-            gw = grp[:].bitcast(F32)
+        def transposes(s, g):
+            if g == 0:
+                grp = gpool.tile([P, G * NODES], BF16, name="grp", align_bytes=64)
+                codes = gpool.tile([P, G * 768], U32, name="codes", align_bytes=64)
+                scales = gpool.tile([P, G * 768], U8, name="scales", align_bytes=64)
+                g_tiles[s] = grp
+                c_tiles[s] = codes
+                s_tiles[s] = scales
+            gw = g_tiles[s][:].bitcast(F32)
             aw = a_tiles[s][:].bitcast(F32)
-            for k in range(BANKS):
-                g, kk = divmod(k, 3)
+            for kk in range(3):
                 tp = transpose_bank(aw, [g * ROWW + (2 * kk + n) * 256 for n in range(2)])
                 copy_bank(tp, gw[:, g * ROWW + kk * 512 : g * ROWW + (kk + 1) * 512])
-            codes = gpool.tile([P, G * 768], U32, name="codes", align_bytes=64)
-            scales = gpool.tile([P, G * 768], U8, name="scales", align_bytes=64)
-            c_tiles[s] = codes
-            s_tiles[s] = scales
 
         def quantise(s, k):
             g, kk = divmod(k, 3)
@@ -218,10 +249,12 @@ def tile_allgnn_pa_kernel(tc, x, adj, W_in, b_in, out):
                 in_=g_tiles[s][:, 4 * w0 : 4 * w0 + 1024],
             )
 
-        def aggregate(s):
-            acc = ps_a.tile([P, 4, HID], F32, name="acc")
-            acc_tiles[s] = acc
-            for g in range(G):
+        def aggregate(s, gs):
+            if gs[0] == 0:
+                acc = ps_a.tile([P, 4, HID], F32, name="acc")
+                acc_tiles[s] = acc
+            acc = acc_tiles[s]
+            for g in gs:
                 for c in range(NPASS):
                     cols = slice(g * 768 + c * P, g * 768 + (c + 1) * P)
                     nc.tensor.matmul_mx(
@@ -301,32 +334,40 @@ def tile_allgnn_pa_kernel(tc, x, adj, W_in, b_in, out):
                 )
             nc.sync.dma_start(out=out_v[s], in_=o_sb[:])
 
-        for tau in range(-1, NS + 1):
-            sp, s0, s1 = tau - 1, tau, tau + 1
-            if has_p(sp):
-                degrees_to_sbuf(sp)
-            if s1 < NS:
+        for tau in range(-1, NS):
+            s0, s1 = tau, tau + 1
+            more = s1 < NS
+            if s0 >= 0:
+                quantise(s0, BANKS - 1)
+            if more:
                 vector_degrees(s1)
-                transposes(s1)
+                transposes(s1, 0)
+            if tau < 0:
+                idle_passes(2)
+            if has_p(s0):
+                tensor_degrees(s0)
+                degrees_to_sbuf(s0)
+            if more:
+                transposes(s1, 1)
                 if s1 + ABUFS < NS:
                     load_adj(s1 + ABUFS)
-            if has_p(sp):
-                fold_degrees(sp)
-            if s1 < NS:
-                quantise(s1, 0)
-                quantise(s1, 1)
-                if not has_p(s1):
-                    reciprocals(s1)
-            if has_p(sp):
-                reciprocals(sp)
-            if s1 < NS:
-                for k in range(2, BANKS):
-                    quantise(s1, k)
-            if 0 <= s0 < NS:
-                aggregate(s0)
+                if tau < 0:
+                    idle_passes(2)
                 if has_p(s0):
-                    tensor_degrees(s0)
-            if has_p(sp):
-                finish(sp)
-            if 0 <= s0 < NS and not has_p(s0):
+                    fold_degrees(s0)
+                for k in range(3):
+                    quantise(s1, k)
+                if s0 >= 0:
+                    reciprocals(s0)
+                for k in range(3, BANKS - 1):
+                    quantise(s1, k)
+                if s0 >= 0:
+                    aggregate(s0, [0, 1])
+            else:
+                aggregate(s0, [0])
+                if has_p(s0):
+                    fold_degrees(s0)
+                reciprocals(s0)
+                aggregate(s0, [1])
+            if s0 >= 0:
                 finish(s0)

@@ -25,10 +25,10 @@ NPASS = NODES // 512
 ROWW = NODES // 2
 BANKS = 3 * G
 ABUFS = 5
-DEGN = 28
+DEGN = 18
 ECOL = 448
 PIN = True
-MODES = ["PV"] * NS
+MODES = ["PP", "PV"] * (NS // 2)
 WARM = 4
 PIECES = {0: 6, 1: 3}
 
@@ -240,13 +240,12 @@ def tile_allgnn_pa_kernel(tc, x, adj, W_in, b_in, out):
                 tp = transpose_bank(aw, [g * ROWW + (2 * kk + n) * 256 for n in range(2)])
                 copy_bank(tp, gw[:, g * ROWW + kk * 512 : g * ROWW + (kk + 1) * 512])
 
-        def quantise(s, k):
-            g, kk = divmod(k, 3)
-            w0 = g * 768 + kk * 256
+        def quantise(s, m):
+            w0 = m * 512
             nc.vector.quantize_mx(
-                out=c_tiles[s][:, w0 : w0 + 256].bitcast(FP8X4),
-                scales=s_tiles[s][:, w0 : w0 + 256],
-                in_=g_tiles[s][:, 4 * w0 : 4 * w0 + 1024],
+                out=c_tiles[s][:, w0 : w0 + 512].bitcast(FP8X4),
+                scales=s_tiles[s][:, w0 : w0 + 512],
+                in_=g_tiles[s][:, 4 * w0 : 4 * w0 + 2048],
             )
 
         def aggregate(s, gs):
@@ -338,7 +337,7 @@ def tile_allgnn_pa_kernel(tc, x, adj, W_in, b_in, out):
             s0, s1 = tau, tau + 1
             more = s1 < NS
             if s0 >= 0:
-                quantise(s0, BANKS - 1)
+                quantise(s0, 2)
             if more:
                 vector_degrees(s1)
                 transposes(s1, 0)
@@ -355,12 +354,10 @@ def tile_allgnn_pa_kernel(tc, x, adj, W_in, b_in, out):
                     idle_passes(2)
                 if has_p(s0):
                     fold_degrees(s0)
-                for k in range(3):
-                    quantise(s1, k)
+                quantise(s1, 0)
                 if s0 >= 0:
                     reciprocals(s0)
-                for k in range(3, BANKS - 1):
-                    quantise(s1, k)
+                quantise(s1, 1)
                 if s0 >= 0:
                     aggregate(s0, [0, 1])
             else:

@@ -30,6 +30,7 @@ ECOL = 448
 PIN = True
 MODES = ["PP", "PV"] * (NS // 2)
 WARM = 4
+V_BANKS = {"PP": (2, 5), "PV": ()}
 PIECES = {0: 6, 1: 3}
 
 
@@ -204,6 +205,7 @@ def tile_allgnn_pa_kernel(tc, x, adj, W_in, b_in, out):
         dsb_tiles = {}
         dp1_tiles = {}
         rec_tiles = {}
+        pending = {}
 
         def p_list(s):
             return [g for g in range(G) if MODES[s][g] == "P"]
@@ -238,7 +240,19 @@ def tile_allgnn_pa_kernel(tc, x, adj, W_in, b_in, out):
             aw = a_tiles[s][:].bitcast(F32)
             for kk in range(3):
                 tp = transpose_bank(aw, [g * ROWW + (2 * kk + n) * 256 for n in range(2)])
-                copy_bank(tp, gw[:, g * ROWW + kk * 512 : g * ROWW + (kk + 1) * 512])
+                dst = gw[:, g * ROWW + kk * 512 : g * ROWW + (kk + 1) * 512]
+                if g * 3 + kk in V_BANKS[MODES[s]]:
+                    pending[(s, g)] = (tp, dst)
+                else:
+                    copy_bank(tp, dst)
+
+        def vector_copy(s, g):
+            if (s, g) in pending:
+                tp, dst = pending[(s, g)]
+                nc.vector.tensor_copy(
+                    out=dst.rearrange("p (n i u) -> p n i u", n=2, i=P, u=2),
+                    in_=tp[:].rearrange("p n u i -> p n i u"),
+                )
 
         def quantise(s, m):
             w0 = m * 512
@@ -341,6 +355,7 @@ def tile_allgnn_pa_kernel(tc, x, adj, W_in, b_in, out):
             if more:
                 vector_degrees(s1)
                 transposes(s1, 0)
+                vector_copy(s1, 0)
             if tau < 0:
                 idle_passes(2)
             if has_p(s0):
@@ -357,6 +372,7 @@ def tile_allgnn_pa_kernel(tc, x, adj, W_in, b_in, out):
                 quantise(s1, 0)
                 if s0 >= 0:
                     reciprocals(s0)
+                vector_copy(s1, 1)
                 quantise(s1, 1)
                 if s0 >= 0:
                     aggregate(s0, [0, 1])

@@ -25,12 +25,14 @@ NPASS = NODES // 512
 ROWW = NODES // 2
 BANKS = 3 * G
 ABUFS = 5
-DEGN = 18
+DEGN = 26
 ECOL = 448
 PIN = True
-MODES = ["PP", "PV"] * (NS // 2)
+MODES = ["PP"] + ["PV"] * (NS - 1)
+IDLE_X = 1
+IDLE_S1 = 1
+IDLE_A0 = 0
 WARM = 4
-V_BANKS = {"PP": (2, 5), "PV": ()}
 PIECES = {0: 6, 1: 3}
 
 
@@ -84,6 +86,8 @@ def tile_allgnn_pa_kernel(tc, x, adj, W_in, b_in, out):
         nc.vector.quantize_mx(out=idle_codes[:].bitcast(FP8X4), scales=idle_scales[:], in_=idle_src[:])
 
         def idle_passes(n):
+            if n == 0:
+                return
             tp = ps_t.tile([P, 2, 2, P], F32, name="tp")
             for i in range(n):
                 nc.tensor.matmul_mx(
@@ -173,7 +177,7 @@ def tile_allgnn_pa_kernel(tc, x, adj, W_in, b_in, out):
                     start=True,
                     stop=True,
                 )
-            idle_passes(1)
+            idle_passes(IDLE_S1)
             hs = slice(c * 512, (c + 1) * 512)
             nc.vector.tensor_tensor(
                 out=h_grp[:, hs].rearrange("p (h t) -> p h t", t=4),
@@ -187,16 +191,6 @@ def tile_allgnn_pa_kernel(tc, x, adj, W_in, b_in, out):
                 in_=h_grp[:, hs],
             )
 
-        for c in range(NPASS + 2):
-            if c < NPASS:
-                stage1_transpose(c)
-                if c < 2:
-                    idle_passes(1)
-            if 0 <= c - 1 < NPASS:
-                stage1_quantise(c - 1)
-            if c - 2 >= 0:
-                stage1_matmul(c - 2)
-
         g_tiles = {}
         c_tiles = {}
         s_tiles = {}
@@ -205,7 +199,6 @@ def tile_allgnn_pa_kernel(tc, x, adj, W_in, b_in, out):
         dsb_tiles = {}
         dp1_tiles = {}
         rec_tiles = {}
-        pending = {}
 
         def p_list(s):
             return [g for g in range(G) if MODES[s][g] == "P"]
@@ -240,19 +233,7 @@ def tile_allgnn_pa_kernel(tc, x, adj, W_in, b_in, out):
             aw = a_tiles[s][:].bitcast(F32)
             for kk in range(3):
                 tp = transpose_bank(aw, [g * ROWW + (2 * kk + n) * 256 for n in range(2)])
-                dst = gw[:, g * ROWW + kk * 512 : g * ROWW + (kk + 1) * 512]
-                if g * 3 + kk in V_BANKS[MODES[s]]:
-                    pending[(s, g)] = (tp, dst)
-                else:
-                    copy_bank(tp, dst)
-
-        def vector_copy(s, g):
-            if (s, g) in pending:
-                tp, dst = pending[(s, g)]
-                nc.vector.tensor_copy(
-                    out=dst.rearrange("p (n i u) -> p n i u", n=2, i=P, u=2),
-                    in_=tp[:].rearrange("p n u i -> p n i u"),
-                )
+                copy_bank(tp, gw[:, g * ROWW + kk * 512 : g * ROWW + (kk + 1) * 512])
 
         def quantise(s, m):
             w0 = m * 512
@@ -300,12 +281,11 @@ def tile_allgnn_pa_kernel(tc, x, adj, W_in, b_in, out):
             npt = len(p_list(s))
             dsb = small.tile([P, 4 * G], F32, name="dsb")
             dsb_tiles[s] = dsb
-            nc.vector.tensor_scalar(
+            nc.scalar.activation(
                 out=dsb[:, 0 : 4 * npt].unsqueeze(2),
-                in0=de_tiles[s][:, 0 : 4 * npt * DEGN].rearrange("p (r n) -> p r n", n=DEGN)[:, :, 0:1],
-                scalar1=0.25,
-                scalar2=None,
-                op0=ALU.add,
+                in_=de_tiles[s][:, 0 : 4 * npt * DEGN].rearrange("p (r n) -> p r n", n=DEGN)[:, :, 0:1],
+                func=ACTF.Copy,
+                bias=0.25,
             )
 
         def fold_degrees(s):
@@ -347,6 +327,18 @@ def tile_allgnn_pa_kernel(tc, x, adj, W_in, b_in, out):
                 )
             nc.sync.dma_start(out=out_v[s], in_=o_sb[:])
 
+        for c in range(NPASS + 2):
+            if c < NPASS:
+                stage1_transpose(c)
+                if c < 2:
+                    idle_passes(IDLE_X)
+            else:
+                transposes(0, c - NPASS)
+            if 0 <= c - 1 < NPASS:
+                stage1_quantise(c - 1)
+            if c - 2 >= 0:
+                stage1_matmul(c - 2)
+
         for tau in range(-1, NS):
             s0, s1 = tau, tau + 1
             more = s1 < NS
@@ -354,25 +346,25 @@ def tile_allgnn_pa_kernel(tc, x, adj, W_in, b_in, out):
                 quantise(s0, 2)
             if more:
                 vector_degrees(s1)
-                transposes(s1, 0)
-                vector_copy(s1, 0)
+                if tau >= 0:
+                    transposes(s1, 0)
             if tau < 0:
-                idle_passes(2)
+                idle_passes(IDLE_A0)
             if has_p(s0):
                 tensor_degrees(s0)
                 degrees_to_sbuf(s0)
             if more:
-                transposes(s1, 1)
+                if tau >= 0:
+                    transposes(s1, 1)
                 if s1 + ABUFS < NS:
                     load_adj(s1 + ABUFS)
                 if tau < 0:
-                    idle_passes(2)
+                    idle_passes(IDLE_A0)
                 if has_p(s0):
                     fold_degrees(s0)
                 quantise(s1, 0)
                 if s0 >= 0:
                     reciprocals(s0)
-                vector_copy(s1, 1)
                 quantise(s1, 1)
                 if s0 >= 0:
                     aggregate(s0, [0, 1])

@@ -29,10 +29,10 @@ DEGN = 26
 ECOL = 448
 PIN = True
 MODES = ["PP"] + ["PV"] * (NS - 1)
-IDLE_X = 1
-IDLE_S1 = 1
+IDLE_X = 0
+IDLE_S1 = 0
 IDLE_A0 = 0
-WARM = 4
+WARM = 0
 PIECES = {0: 6, 1: 3}
 
 

@@ -26,13 +26,9 @@ ROWW = NODES // 2
 BANKS = 3 * G
 ABUFS = 5
 DEGN = 26
-ECOL = 448
+NPIECE = 3
 PIN = True
 MODES = ["PP"] + ["PV"] * (NS - 1)
-IDLE_X = 0
-IDLE_S1 = 0
-IDLE_A0 = 0
-WARM = 0
 PIECES = {0: 6, 1: 3}
 
 
@@ -79,28 +75,6 @@ def tile_allgnn_pa_kernel(tc, x, adj, W_in, b_in, out):
         for s in range(ABUFS):
             load_adj(s)
 
-        idle_codes = const.tile([P, 512], U32, align_bytes=64)
-        idle_scales = const.tile([P, 512], U8, align_bytes=64)
-        idle_src = const.tile([P, 2048], BF16, align_bytes=64)
-        nc.vector.memset(idle_src[:].bitcast(I32), 0)
-        nc.vector.quantize_mx(out=idle_codes[:].bitcast(FP8X4), scales=idle_scales[:], in_=idle_src[:])
-
-        def idle_passes(n):
-            if n == 0:
-                return
-            tp = ps_t.tile([P, 2, 2, P], F32, name="tp")
-            for i in range(n):
-                nc.tensor.matmul_mx(
-                    out=tp[:].rearrange("p a b c -> p (a b c)"),
-                    lhsT=idle_codes[:, 0:P].bitcast(FP8X4),
-                    lhsT_scale=idle_scales[:, 0:P],
-                    rhs=idle_codes[:].bitcast(FP8X4),
-                    rhs_scale=idle_scales[:],
-                    start=True,
-                    stop=True,
-                )
-
-        idle_passes(WARM)
         ident = const.tile([P, P], F32)
         make_identity(nc, ident[:])
         ones = const.tile([P, DEGN], BF16)
@@ -109,7 +83,7 @@ def tile_allgnn_pa_kernel(tc, x, adj, W_in, b_in, out):
         nc.vector.tensor_reduce(
             out=fold_q[:], in_=ident[:].rearrange("p (q t) -> p q t", t=4), axis=AX.X, op=ALU.add
         )
-        fold = const.tile([P, 4, 32], F32)
+        fold = const.tile([P, 4, 32], BF16)
         nc.vector.tensor_copy(out=fold[:], in_=fold_q[:].unsqueeze(1).to_broadcast([P, 4, 32]))
         quad = const.tile([P, 4], F32)
         nc.vector.tensor_reduce(
@@ -177,7 +151,6 @@ def tile_allgnn_pa_kernel(tc, x, adj, W_in, b_in, out):
                     start=True,
                     stop=True,
                 )
-            idle_passes(IDLE_S1)
             hs = slice(c * 512, (c + 1) * 512)
             nc.vector.tensor_tensor(
                 out=h_grp[:, hs].rearrange("p (h t) -> p h t", t=4),
@@ -199,12 +172,10 @@ def tile_allgnn_pa_kernel(tc, x, adj, W_in, b_in, out):
         dsb_tiles = {}
         dp1_tiles = {}
         rec_tiles = {}
+        pieces_tiles = {}
 
         def p_list(s):
             return [g for g in range(G) if MODES[s][g] == "P"]
-
-        def has_p(s):
-            return 0 <= s < NS and len(p_list(s)) > 0
 
         def vector_degrees(s):
             dp1 = small.tile([P, G], F32, name="dp1")
@@ -243,12 +214,13 @@ def tile_allgnn_pa_kernel(tc, x, adj, W_in, b_in, out):
                 in_=g_tiles[s][:, 4 * w0 : 4 * w0 + 2048],
             )
 
-        def aggregate(s, gs):
-            if gs[0] == 0:
-                acc = ps_a.tile([P, 4, HID], F32, name="acc")
-                acc_tiles[s] = acc
+        def open_acc(s):
+            acc = ps_a.tile([P, 4, HID], F32, name="acc")
+            acc_tiles[s] = acc
+
+        def aggregate(s):
             acc = acc_tiles[s]
-            for g in gs:
+            for g in range(G):
                 for c in range(NPASS):
                     cols = slice(g * 768 + c * P, g * 768 + (c + 1) * P)
                     nc.tensor.matmul_mx(
@@ -288,30 +260,45 @@ def tile_allgnn_pa_kernel(tc, x, adj, W_in, b_in, out):
                 bias=0.25,
             )
 
+        def split_degrees(s):
+            w = 4 * len(p_list(s))
+            d = dsb_tiles[s]
+            pieces = small.tile([P, NPIECE, 4 * G], BF16, name="pieces")
+            pieces_tiles[s] = pieces
+            rest = small.tile([P, 4 * G], F32, name="rest")
+            nc.gpsimd.tensor_copy(out=pieces[:, 0, 0:w], in_=d[:, 0:w])
+            nc.gpsimd.tensor_tensor(out=rest[:, 0:w], in0=d[:, 0:w], in1=pieces[:, 0, 0:w], op=ALU.subtract)
+            nc.gpsimd.tensor_copy(out=pieces[:, 1, 0:w], in_=rest[:, 0:w])
+            nc.gpsimd.tensor_tensor(
+                out=pieces[:, 2, 0:w], in0=rest[:, 0:w], in1=pieces[:, 1, 0:w], op=ALU.subtract
+            )
+
         def fold_degrees(s):
-            npt = len(p_list(s))
+            w = 4 * len(p_list(s))
             nc.tensor.matmul(
-                out=de_tiles[s][:, ECOL : ECOL + 4 * npt],
+                out=acc_tiles[s][:, 2, 0 : NPIECE * w].rearrange("p (k w) -> p k w", w=w),
                 lhsT=fold[:].rearrange("p r q -> p (r q)"),
-                rhs=dsb_tiles[s][:, 0 : 4 * npt],
+                rhs=pieces_tiles[s][:, :, 0:w],
                 start=True,
                 stop=True,
             )
 
+        def pick_degrees(s):
+            w = 4 * len(p_list(s))
+            folded = acc_tiles[s][:, 2, 0 : NPIECE * w].rearrange("p (k w) -> p k w", w=w)
+            for n, g in enumerate(p_list(s)):
+                pick = small.tile([P, NPIECE, 4], F32, name="pick")
+                nc.vector.scalar_tensor_tensor(
+                    out=pick[:],
+                    in0=folded[:, :, 4 * n : 4 * n + 4],
+                    scalar=1.0,
+                    in1=quad[:].unsqueeze(1).to_broadcast([P, NPIECE, 4]),
+                    op0=ALU.mult,
+                    op1=ALU.mult,
+                    accum_out=dp1_tiles[s][:, g : g + 1],
+                )
+
         def reciprocals(s):
-            pl = p_list(s)
-            npt = len(pl)
-            if npt > 0:
-                pick = small.tile([P, G, 4], F32, name="pick")
-                nc.vector.tensor_tensor(
-                    out=pick[:, 0:npt, :],
-                    in0=de_tiles[s][:, ECOL : ECOL + 4 * npt].rearrange("p (n r) -> p n r", r=4),
-                    in1=quad[:].unsqueeze(1).to_broadcast([P, npt, 4]),
-                    op=ALU.mult,
-                )
-                nc.vector.tensor_reduce(
-                    out=dp1_tiles[s][:, pl[0] : pl[0] + npt], in_=pick[:, 0:npt, :], axis=AX.X, op=ALU.add
-                )
             rec = small.tile([P, G], F32, name="rec")
             rec_tiles[s] = rec
             nc.vector.reciprocal(out=rec[:], in_=dp1_tiles[s][:])
@@ -330,8 +317,6 @@ def tile_allgnn_pa_kernel(tc, x, adj, W_in, b_in, out):
         for c in range(NPASS + 2):
             if c < NPASS:
                 stage1_transpose(c)
-                if c < 2:
-                    idle_passes(IDLE_X)
             else:
                 transposes(0, c - NPASS)
             if 0 <= c - 1 < NPASS:
@@ -340,39 +325,35 @@ def tile_allgnn_pa_kernel(tc, x, adj, W_in, b_in, out):
                 stage1_matmul(c - 2)
 
         for tau in range(-1, NS):
-            s0, s1 = tau, tau + 1
+            sp, s0, s1 = tau - 1, tau, tau + 1
             more = s1 < NS
+            if more and s0 >= 0:
+                transposes(s1, 0)
+            if sp >= 0:
+                fold_degrees(sp)
+                pick_degrees(sp)
             if s0 >= 0:
                 quantise(s0, 2)
-            if more:
-                vector_degrees(s1)
-                if tau >= 0:
-                    transposes(s1, 0)
-            if tau < 0:
-                idle_passes(IDLE_A0)
-            if has_p(s0):
+            if sp >= 0:
+                reciprocals(sp)
+            if s0 >= 0:
                 tensor_degrees(s0)
                 degrees_to_sbuf(s0)
+                split_degrees(s0)
+            if sp >= 0:
+                finish(sp)
             if more:
-                if tau >= 0:
+                vector_degrees(s1)
+                if s0 >= 0:
                     transposes(s1, 1)
                 if s1 + ABUFS < NS:
                     load_adj(s1 + ABUFS)
-                if tau < 0:
-                    idle_passes(IDLE_A0)
-                if has_p(s0):
-                    fold_degrees(s0)
                 quantise(s1, 0)
-                if s0 >= 0:
-                    reciprocals(s0)
                 quantise(s1, 1)
-                if s0 >= 0:
-                    aggregate(s0, [0, 1])
-            else:
-                aggregate(s0, [0])
-                if has_p(s0):
-                    fold_degrees(s0)
-                reciprocals(s0)
-                aggregate(s0, [1])
             if s0 >= 0:
-                finish(s0)
+                open_acc(s0)
+                aggregate(s0)
+        fold_degrees(NS - 1)
+        pick_degrees(NS - 1)
+        reciprocals(NS - 1)
+        finish(NS - 1)

@@ -26,9 +26,8 @@ ROWW = NODES // 2
 BANKS = 3 * G
 ABUFS = 5
 DEGN = 26
-NPIECE = 3
 PIN = True
-MODES = ["PP"] + ["PV"] * (NS - 1)
+MODES = ["PP"] + ["PV"] * 5 + ["PP", "VV"] * 3
 PIECES = {0: 6, 1: 3}
 
 
@@ -43,9 +42,9 @@ def tile_allgnn_pa_kernel(tc, x, adj, W_in, b_in, out):
         const = ctx.enter_context(tc.tile_pool(name="const", bufs=1))
         apool = ctx.enter_context(tc.tile_pool(name="apool", bufs=ABUFS))
         gpool = ctx.enter_context(tc.tile_pool(name="gpool", bufs=3))
-        small = ctx.enter_context(tc.tile_pool(name="small", bufs=4))
-        ps_t = ctx.enter_context(tc.psum_pool(name="ps_t", bufs=6))
-        ps_a = ctx.enter_context(tc.psum_pool(name="ps_a", bufs=1))
+        small = ctx.enter_context(tc.tile_pool(name="small", bufs=5))
+        ps_t = ctx.enter_context(tc.psum_pool(name="ps_t", bufs=5))
+        ps_a = ctx.enter_context(tc.psum_pool(name="ps_a", bufs=2))
         ps_d = ctx.enter_context(tc.psum_pool(name="ps_d", bufs=1))
         if PIN:
             ctx.enter_context(tc.manual_schedule())
@@ -83,7 +82,7 @@ def tile_allgnn_pa_kernel(tc, x, adj, W_in, b_in, out):
         nc.vector.tensor_reduce(
             out=fold_q[:], in_=ident[:].rearrange("p (q t) -> p q t", t=4), axis=AX.X, op=ALU.add
         )
-        fold = const.tile([P, 4, 32], BF16)
+        fold = const.tile([P, 4, 32], F32)
         nc.vector.tensor_copy(out=fold[:], in_=fold_q[:].unsqueeze(1).to_broadcast([P, 4, 32]))
         quad = const.tile([P, 4], F32)
         nc.vector.tensor_reduce(
@@ -151,6 +150,9 @@ def tile_allgnn_pa_kernel(tc, x, adj, W_in, b_in, out):
                     start=True,
                     stop=True,
                 )
+            return ps1
+
+        def stage1_bias(c, ps1):
             hs = slice(c * 512, (c + 1) * 512)
             nc.vector.tensor_tensor(
                 out=h_grp[:, hs].rearrange("p (h t) -> p h t", t=4),
@@ -158,6 +160,9 @@ def tile_allgnn_pa_kernel(tc, x, adj, W_in, b_in, out):
                 in1=bias[:].unsqueeze(2).to_broadcast([P, HID, 4]),
                 op=ALU.add,
             )
+
+        def stage1_quantise_h(c):
+            hs = slice(c * 512, (c + 1) * 512)
             nc.vector.quantize_mx(
                 out=h_codes[:, c * HID : (c + 1) * HID].bitcast(FP8X4),
                 scales=h_scales[:, c * HID : (c + 1) * HID],
@@ -172,25 +177,33 @@ def tile_allgnn_pa_kernel(tc, x, adj, W_in, b_in, out):
         dsb_tiles = {}
         dp1_tiles = {}
         rec_tiles = {}
-        pieces_tiles = {}
 
         def p_list(s):
+            if s < 0:
+                return []
             return [g for g in range(G) if MODES[s][g] == "P"]
 
-        def vector_degrees(s):
-            dp1 = small.tile([P, G], F32, name="dp1")
-            dp1_tiles[s] = dp1
+        v_plan = {}
+        for s in range(NS):
             for g in range(G):
                 if MODES[s][g] == "V":
-                    nc.vector.tensor_scalar(
-                        out=junk[:],
-                        in0=a_tiles[s][:, g * NODES : (g + 1) * NODES],
-                        scalar1=1.0,
-                        scalar2=1.0,
-                        op0=ALU.mult,
-                        op1=ALU.add,
-                        accum_out=dp1[:, g : g + 1],
-                    )
+                    turn = s - 1 if MODES[s] == "VV" and g == 0 else s
+                    v_plan.setdefault(turn, []).append((s, g))
+
+        def open_degrees(s):
+            dp1 = small.tile([P, G], F32, name="dp1")
+            dp1_tiles[s] = dp1
+
+        def vector_degrees(s, g):
+            nc.vector.tensor_scalar(
+                out=junk[:],
+                in0=a_tiles[s][:, g * NODES : (g + 1) * NODES],
+                scalar1=1.0,
+                scalar2=1.0,
+                op0=ALU.mult,
+                op1=ALU.add,
+                accum_out=dp1_tiles[s][:, g : g + 1],
+            )
 
         def transposes(s, g):
             if g == 0:
@@ -260,39 +273,24 @@ def tile_allgnn_pa_kernel(tc, x, adj, W_in, b_in, out):
                 bias=0.25,
             )
 
-        def split_degrees(s):
-            w = 4 * len(p_list(s))
-            d = dsb_tiles[s]
-            pieces = small.tile([P, NPIECE, 4 * G], BF16, name="pieces")
-            pieces_tiles[s] = pieces
-            rest = small.tile([P, 4 * G], F32, name="rest")
-            nc.gpsimd.tensor_copy(out=pieces[:, 0, 0:w], in_=d[:, 0:w])
-            nc.gpsimd.tensor_tensor(out=rest[:, 0:w], in0=d[:, 0:w], in1=pieces[:, 0, 0:w], op=ALU.subtract)
-            nc.gpsimd.tensor_copy(out=pieces[:, 1, 0:w], in_=rest[:, 0:w])
-            nc.gpsimd.tensor_tensor(
-                out=pieces[:, 2, 0:w], in0=rest[:, 0:w], in1=pieces[:, 1, 0:w], op=ALU.subtract
-            )
-
         def fold_degrees(s):
             w = 4 * len(p_list(s))
             nc.tensor.matmul(
-                out=acc_tiles[s][:, 2, 0 : NPIECE * w].rearrange("p (k w) -> p k w", w=w),
+                out=acc_tiles[s][:, 2, 0:w],
                 lhsT=fold[:].rearrange("p r q -> p (r q)"),
-                rhs=pieces_tiles[s][:, :, 0:w],
+                rhs=dsb_tiles[s][:, 0:w],
                 start=True,
                 stop=True,
             )
 
         def pick_degrees(s):
-            w = 4 * len(p_list(s))
-            folded = acc_tiles[s][:, 2, 0 : NPIECE * w].rearrange("p (k w) -> p k w", w=w)
             for n, g in enumerate(p_list(s)):
-                pick = small.tile([P, NPIECE, 4], F32, name="pick")
+                pick = small.tile([P, 4], F32, name="pick")
                 nc.vector.scalar_tensor_tensor(
                     out=pick[:],
-                    in0=folded[:, :, 4 * n : 4 * n + 4],
+                    in0=acc_tiles[s][:, 2, 4 * n : 4 * n + 4],
                     scalar=1.0,
-                    in1=quad[:].unsqueeze(1).to_broadcast([P, NPIECE, 4]),
+                    in1=quad[:],
                     op0=ALU.mult,
                     op1=ALU.mult,
                     accum_out=dp1_tiles[s][:, g : g + 1],
@@ -314,46 +312,53 @@ def tile_allgnn_pa_kernel(tc, x, adj, W_in, b_in, out):
                 )
             nc.sync.dma_start(out=out_v[s], in_=o_sb[:])
 
-        for c in range(NPASS + 2):
+        ps1_tiles = {}
+        for c in range(NPASS + 3):
             if c < NPASS:
                 stage1_transpose(c)
-            else:
+            elif c < NPASS + G:
                 transposes(0, c - NPASS)
             if 0 <= c - 1 < NPASS:
                 stage1_quantise(c - 1)
-            if c - 2 >= 0:
-                stage1_matmul(c - 2)
+            if 0 <= c - 2 < NPASS:
+                ps1_tiles[c - 2] = stage1_matmul(c - 2)
+                stage1_bias(c - 2, ps1_tiles[c - 2])
+            if 0 <= c - 3 < NPASS:
+                stage1_quantise_h(c - 3)
 
+        open_degrees(0)
         for tau in range(-1, NS):
             sp, s0, s1 = tau - 1, tau, tau + 1
             more = s1 < NS
             if more and s0 >= 0:
                 transposes(s1, 0)
-            if sp >= 0:
-                fold_degrees(sp)
-                pick_degrees(sp)
+                transposes(s1, 1)
             if s0 >= 0:
                 quantise(s0, 2)
-            if sp >= 0:
-                reciprocals(sp)
-            if s0 >= 0:
+            if p_list(sp):
+                fold_degrees(sp)
+            if p_list(s0):
                 tensor_degrees(s0)
-                degrees_to_sbuf(s0)
-                split_degrees(s0)
-            if sp >= 0:
-                finish(sp)
-            if more:
-                vector_degrees(s1)
-                if s0 >= 0:
-                    transposes(s1, 1)
-                if s1 + ABUFS < NS:
-                    load_adj(s1 + ABUFS)
-                quantise(s1, 0)
-                quantise(s1, 1)
             if s0 >= 0:
                 open_acc(s0)
                 aggregate(s0)
-        fold_degrees(NS - 1)
-        pick_degrees(NS - 1)
+            if s1 + 1 < NS:
+                open_degrees(s1 + 1)
+            for s, g in v_plan.get(s1, []):
+                vector_degrees(s, g)
+            if p_list(sp):
+                pick_degrees(sp)
+            if more:
+                if s1 + ABUFS < NS:
+                    load_adj(s1 + ABUFS)
+                quantise(s1, 0)
+            if sp >= 0:
+                reciprocals(sp)
+            if more:
+                quantise(s1, 1)
+            if p_list(s0):
+                degrees_to_sbuf(s0)
+            if sp >= 0:
+                finish(sp)
         reciprocals(NS - 1)
         finish(NS - 1)

@@ -51,10 +51,13 @@ def tile_allgnn_pa_kernel(tc, x, adj, W_in, b_in, out):
 
         w_raw = const.tile([P, 4 * HID], BF16)
         nc.scalar.dma_start(out=w_raw[:].rearrange("p (u f) -> p u f", u=2), in_=w_v)
-        bias = const.tile([P, HID], BF16)
-        nc.scalar.dma_start(out=bias[:], in_=b_in.partition_broadcast(P))
+        b_row = const.tile([P, HID], BF16)
+        nc.vector.memset(b_row[:].bitcast(I32), 0)
+        nc.scalar.dma_start(out=b_row[0:1, :], in_=b_in.unsqueeze(0))
         x_sb = const.tile([P, NPASS * 2048], BF16)
-        for c in range(NPASS):
+        for u in range(2):
+            nc.sync.dma_start(out=x_sb[:, u * 1024 : (u + 1) * 1024], in_=x_v[0][:, u, :])
+        for c in range(1, NPASS):
             nc.sync.dma_start(
                 out=x_sb[:, c * 2048 : (c + 1) * 2048].rearrange("p (u f) -> p u f", u=2),
                 in_=x_v[c],
@@ -76,7 +79,7 @@ def tile_allgnn_pa_kernel(tc, x, adj, W_in, b_in, out):
 
         ident = const.tile([P, P], F32)
         make_identity(nc, ident[:])
-        ones = const.tile([P, DEGN], BF16)
+        ones = const.tile([P, P], BF16)
         nc.vector.memset(ones[:], 1.0)
         fold_q = const.tile([P, 32], F32)
         nc.vector.tensor_reduce(
@@ -118,6 +121,13 @@ def tile_allgnn_pa_kernel(tc, x, adj, W_in, b_in, out):
                 out=dst_words.rearrange("p (n i u) -> p n i u", n=2, i=P, u=2),
                 in_=tp[:].rearrange("p n u i -> p n i u"),
             )
+
+        bias = const.tile([P, HID], BF16)
+
+        def spread_bias():
+            bb = ps_d.tile([P, 512], F32, name="de")
+            nc.tensor.matmul(out=bb[:, 0:HID], lhsT=ones[:], rhs=b_row[:], start=True, stop=True)
+            nc.vector.tensor_copy(out=bias[:], in_=bb[:, 0:HID])
 
         x_words = x_sb[:].bitcast(F32)
         gx_tiles = {}
@@ -257,7 +267,7 @@ def tile_allgnn_pa_kernel(tc, x, adj, W_in, b_in, out):
                         nc.tensor.matmul(
                             out=de[:, col : col + DEGN],
                             lhsT=g_tiles[s][:, o : o + P],
-                            rhs=ones[:],
+                            rhs=ones[:, 0:DEGN],
                             start=(c == 0),
                             stop=(c == NPASS - 1),
                         )
@@ -316,6 +326,8 @@ def tile_allgnn_pa_kernel(tc, x, adj, W_in, b_in, out):
         for c in range(NPASS + 3):
             if c < NPASS:
                 stage1_transpose(c)
+                if c == 0:
+                    spread_bias()
             elif c < NPASS + G:
                 transposes(0, c - NPASS)
             if 0 <= c - 1 < NPASS:

@@ -344,33 +344,33 @@ def tile_allgnn_pa_kernel(tc, x, adj, W_in, b_in, out):
             more = s1 < NS
             if more and s0 >= 0:
                 transposes(s1, 0)
-                transposes(s1, 1)
             if s0 >= 0:
                 quantise(s0, 2)
-            if p_list(sp):
-                fold_degrees(sp)
+            if sp >= 0:
+                reciprocals(sp)
             if p_list(s0):
                 tensor_degrees(s0)
-            if s0 >= 0:
-                open_acc(s0)
-                aggregate(s0)
+                degrees_to_sbuf(s0)
+            if sp >= 0:
+                finish(sp)
             if s1 + 1 < NS:
                 open_degrees(s1 + 1)
             for s, g in v_plan.get(s1, []):
                 vector_degrees(s, g)
-            if p_list(sp):
-                pick_degrees(sp)
             if more:
+                if s0 >= 0:
+                    transposes(s1, 1)
                 if s1 + ABUFS < NS:
                     load_adj(s1 + ABUFS)
                 quantise(s1, 0)
-            if sp >= 0:
-                reciprocals(sp)
+            if s0 >= 0:
+                open_acc(s0)
+                aggregate(s0)
+            if p_list(s0):
+                fold_degrees(s0)
             if more:
                 quantise(s1, 1)
             if p_list(s0):
-                degrees_to_sbuf(s0)
-            if sp >= 0:
-                finish(sp)
+                pick_degrees(s0)
         reciprocals(NS - 1)
         finish(NS - 1)

@@ -27,8 +27,8 @@ BANKS = 3 * G
 ABUFS = 5
 DEGN = 26
 PIN = True
-MODES = ["PP"] + ["PV"] * 5 + ["PP", "VV"] * 3
-PIECES = {0: 6, 1: 3}
+MODES = ["PP"] + ["PV"] * 3 + ["PP", "VV"] * 4
+PIECES = {0: 2, 1: 3}
 
 
 def tile_allgnn_pa_kernel(tc, x, adj, W_in, b_in, out):
@@ -50,13 +50,13 @@ def tile_allgnn_pa_kernel(tc, x, adj, W_in, b_in, out):
             ctx.enter_context(tc.manual_schedule())
 
         w_raw = const.tile([P, 4 * HID], BF16)
-        nc.scalar.dma_start(out=w_raw[:].rearrange("p (u f) -> p u f", u=2), in_=w_v)
         b_row = const.tile([P, HID], BF16)
         nc.vector.memset(b_row[:].bitcast(I32), 0)
         nc.scalar.dma_start(out=b_row[0:1, :], in_=b_in.unsqueeze(0))
         x_sb = const.tile([P, NPASS * 2048], BF16)
         for u in range(2):
             nc.sync.dma_start(out=x_sb[:, u * 1024 : (u + 1) * 1024], in_=x_v[0][:, u, :])
+        nc.sync.dma_start(out=w_raw[:].rearrange("p (u f) -> p u f", u=2), in_=w_v)
         for c in range(1, NPASS):
             nc.sync.dma_start(
                 out=x_sb[:, c * 2048 : (c + 1) * 2048].rearrange("p (u f) -> p u f", u=2),
@@ -229,13 +229,19 @@ def tile_allgnn_pa_kernel(tc, x, adj, W_in, b_in, out):
                 tp = transpose_bank(aw, [g * ROWW + (2 * kk + n) * 256 for n in range(2)])
                 copy_bank(tp, gw[:, g * ROWW + kk * 512 : g * ROWW + (kk + 1) * 512])
 
-        def quantise(s, m):
-            w0 = m * 512
+        def quantise_words(s, w0, w1):
             nc.vector.quantize_mx(
-                out=c_tiles[s][:, w0 : w0 + 512].bitcast(FP8X4),
-                scales=s_tiles[s][:, w0 : w0 + 512],
-                in_=g_tiles[s][:, 4 * w0 : 4 * w0 + 2048],
+                out=c_tiles[s][:, w0:w1].bitcast(FP8X4),
+                scales=s_tiles[s][:, w0:w1],
+                in_=g_tiles[s][:, 4 * w0 : 4 * w1],
             )
+
+        def quantise(s, m):
+            if s == NS - 1 and m == 2:
+                quantise_words(s, 1024, 1280)
+                quantise_words(s, 1280, 1536)
+            else:
+                quantise_words(s, m * 512, m * 512 + 512)
 
         def open_acc(s):
             acc = ps_a.tile([P, 4, HID], F32, name="acc")
@@ -320,7 +326,11 @@ def tile_allgnn_pa_kernel(tc, x, adj, W_in, b_in, out):
                     func=ACTF.Copy,
                     scale=rec_tiles[s][:, g : g + 1],
                 )
-            nc.sync.dma_start(out=out_v[s], in_=o_sb[:])
+                if s == NS - 1:
+                    cols = slice(g * HID, (g + 1) * HID)
+                    nc.sync.dma_start(out=out_v[s][:, cols], in_=o_sb[:, cols])
+            if s < NS - 1:
+                nc.sync.dma_start(out=out_v[s], in_=o_sb[:])
 
         ps1_tiles = {}
         for c in range(NPASS + 3):

@@ -26,9 +26,10 @@ ROWW = NODES // 2
 BANKS = 3 * G
 ABUFS = 5
 DEGN = 26
+FOLD = 256
 PIN = True
-MODES = ["PP"] + ["PV"] * 3 + ["PP", "VV"] * 4
-PIECES = {0: 2, 1: 3}
+MODES = ["PP", "VV"] * 6
+HALVES = 4
 
 
 def tile_allgnn_pa_kernel(tc, x, adj, W_in, b_in, out):
@@ -56,17 +57,18 @@ def tile_allgnn_pa_kernel(tc, x, adj, W_in, b_in, out):
         x_sb = const.tile([P, NPASS * 2048], BF16)
         for u in range(2):
             nc.sync.dma_start(out=x_sb[:, u * 1024 : (u + 1) * 1024], in_=x_v[0][:, u, :])
-        nc.sync.dma_start(out=w_raw[:].rearrange("p (u f) -> p u f", u=2), in_=w_v)
         for c in range(1, NPASS):
             nc.sync.dma_start(
                 out=x_sb[:, c * 2048 : (c + 1) * 2048].rearrange("p (u f) -> p u f", u=2),
                 in_=x_v[c],
             )
+            if c == 1:
+                nc.sync.dma_start(out=w_raw[:].rearrange("p (u f) -> p u f", u=2), in_=w_v)
         a_tiles = {}
 
         def load_adj(s):
             a_sb = apool.tile([P, G * NODES], BF16, name="a_sb")
-            n_piece = PIECES.get(s, 1)
+            n_piece = G if s < HALVES else 1
             width = G * NODES // n_piece
             for i in range(n_piece):
                 nc.sync.dma_start(
@@ -94,13 +96,15 @@ def tile_allgnn_pa_kernel(tc, x, adj, W_in, b_in, out):
         junk = const.tile([P, NODES], BF16)
 
         w_grp = const.tile([P, 4 * HID], BF16, align_bytes=64)
-        nc.vector.tensor_copy(
-            out=w_grp[:].rearrange("p (h t) -> p h t", t=4),
-            in_=w_raw[:].rearrange("p (t h) -> p h t", t=4),
-        )
         w_codes = const.tile([P, HID], U32, align_bytes=64)
         w_scales = const.tile([P, HID], U8, align_bytes=64)
-        nc.vector.quantize_mx(out=w_codes[:].bitcast(FP8X4), scales=w_scales[:], in_=w_grp[:])
+
+        def weights():
+            nc.vector.tensor_copy(
+                out=w_grp[:].rearrange("p (h t) -> p h t", t=4),
+                in_=w_raw[:].rearrange("p (t h) -> p h t", t=4),
+            )
+            nc.vector.quantize_mx(out=w_codes[:].bitcast(FP8X4), scales=w_scales[:], in_=w_grp[:])
 
         x_codes = const.tile([P, NPASS * 512], U32, align_bytes=64)
         x_scales = const.tile([P, NPASS * 512], U8, align_bytes=64)
@@ -187,6 +191,7 @@ def tile_allgnn_pa_kernel(tc, x, adj, W_in, b_in, out):
         dsb_tiles = {}
         dp1_tiles = {}
         rec_tiles = {}
+        pick_tiles = {}
 
         def p_list(s):
             if s < 0:
@@ -229,19 +234,12 @@ def tile_allgnn_pa_kernel(tc, x, adj, W_in, b_in, out):
                 tp = transpose_bank(aw, [g * ROWW + (2 * kk + n) * 256 for n in range(2)])
                 copy_bank(tp, gw[:, g * ROWW + kk * 512 : g * ROWW + (kk + 1) * 512])
 
-        def quantise_words(s, w0, w1):
+        def quantise(s, w0, w1):
             nc.vector.quantize_mx(
                 out=c_tiles[s][:, w0:w1].bitcast(FP8X4),
                 scales=s_tiles[s][:, w0:w1],
                 in_=g_tiles[s][:, 4 * w0 : 4 * w1],
             )
-
-        def quantise(s, m):
-            if s == NS - 1 and m == 2:
-                quantise_words(s, 1024, 1280)
-                quantise_words(s, 1280, 1536)
-            else:
-                quantise_words(s, m * 512, m * 512 + 512)
 
         def open_acc(s):
             acc = ps_a.tile([P, 4, HID], F32, name="acc")
@@ -292,7 +290,7 @@ def tile_allgnn_pa_kernel(tc, x, adj, W_in, b_in, out):
         def fold_degrees(s):
             w = 4 * len(p_list(s))
             nc.tensor.matmul(
-                out=acc_tiles[s][:, 2, 0:w],
+                out=de_tiles[s][:, FOLD : FOLD + w],
                 lhsT=fold[:].rearrange("p r q -> p (r q)"),
                 rhs=dsb_tiles[s][:, 0:w],
                 start=True,
@@ -300,17 +298,24 @@ def tile_allgnn_pa_kernel(tc, x, adj, W_in, b_in, out):
             )
 
         def pick_degrees(s):
-            for n, g in enumerate(p_list(s)):
-                pick = small.tile([P, 4], F32, name="pick")
-                nc.vector.scalar_tensor_tensor(
-                    out=pick[:],
-                    in0=acc_tiles[s][:, 2, 4 * n : 4 * n + 4],
-                    scalar=1.0,
-                    in1=quad[:],
-                    op0=ALU.mult,
-                    op1=ALU.mult,
-                    accum_out=dp1_tiles[s][:, g : g + 1],
-                )
+            w = 4 * len(p_list(s))
+            pick = small.tile([P, 4 * G], F32, name="pick")
+            pick_tiles[s] = pick
+            nc.vector.tensor_tensor(
+                out=pick[:, 0:w].rearrange("p (n r) -> p n r", r=4),
+                in0=de_tiles[s][:, FOLD : FOLD + w].rearrange("p (n r) -> p n r", r=4),
+                in1=quad[:].unsqueeze(1).to_broadcast([P, w // 4, 4]),
+                op=ALU.mult,
+            )
+
+        def sum_picked(s):
+            gs = p_list(s)
+            nc.vector.tensor_reduce(
+                out=dp1_tiles[s][:, gs[0] : gs[-1] + 1],
+                in_=pick_tiles[s][:, 0 : 4 * len(gs)].rearrange("p (n r) -> p n r", r=4),
+                axis=AX.X,
+                op=ALU.add,
+            )
 
         def reciprocals(s):
             rec = small.tile([P, G], F32, name="rec")
@@ -342,6 +347,8 @@ def tile_allgnn_pa_kernel(tc, x, adj, W_in, b_in, out):
                 transposes(0, c - NPASS)
             if 0 <= c - 1 < NPASS:
                 stage1_quantise(c - 1)
+            if c == 1:
+                weights()
             if 0 <= c - 2 < NPASS:
                 ps1_tiles[c - 2] = stage1_matmul(c - 2)
                 stage1_bias(c - 2, ps1_tiles[c - 2])
@@ -354,33 +361,42 @@ def tile_allgnn_pa_kernel(tc, x, adj, W_in, b_in, out):
             more = s1 < NS
             if more and s0 >= 0:
                 transposes(s1, 0)
-            if s0 >= 0:
-                quantise(s0, 2)
+            if more and s0 >= 0:
+                quantise(s0, 1024, 1536)
+            if s0 == NS - 1:
+                quantise(s0, 1024, 1280)
+                reciprocals(s0)
             if sp >= 0:
                 reciprocals(sp)
+            if s0 == NS - 1:
+                quantise(s0, 1280, 1536)
             if p_list(s0):
                 tensor_degrees(s0)
                 degrees_to_sbuf(s0)
-            if sp >= 0:
-                finish(sp)
             if s1 + 1 < NS:
                 open_degrees(s1 + 1)
             for s, g in v_plan.get(s1, []):
                 vector_degrees(s, g)
+            if sp >= 0 and s1 >= NS - 1:
+                finish(sp)
+            if more and s0 >= 0:
+                transposes(s1, 1)
+            if sp >= 0 and s1 < NS - 1:
+                finish(sp)
+            if s1 + ABUFS < NS:
+                load_adj(s1 + ABUFS)
             if more:
-                if s0 >= 0:
-                    transposes(s1, 1)
-                if s1 + ABUFS < NS:
-                    load_adj(s1 + ABUFS)
-                quantise(s1, 0)
+                quantise(s1, 0, 512)
             if s0 >= 0:
                 open_acc(s0)
-                aggregate(s0)
             if p_list(s0):
                 fold_degrees(s0)
-            if more:
-                quantise(s1, 1)
+            if s0 >= 0:
+                aggregate(s0)
             if p_list(s0):
                 pick_degrees(s0)
-        reciprocals(NS - 1)
+            if more:
+                quantise(s1, 512, 1024)
+            if p_list(s0):
+                sum_picked(s0)
         finish(NS - 1)

@@ -24,7 +24,7 @@ NS = NODES // (P * G)
 NPASS = NODES // 512
 ROWW = NODES // 2
 BANKS = 3 * G
-ABUFS = 5
+ABUFS = 8
 DEGN = 26
 FOLD = 256
 PIN = True
@@ -202,7 +202,10 @@ def tile_allgnn_pa_kernel(tc, x, adj, W_in, b_in, out):
         for s in range(NS):
             for g in range(G):
                 if MODES[s][g] == "V":
-                    turn = s - 1 if MODES[s] == "VV" and g == 0 else s
+                    if MODES[s] == "VV":
+                        turn = s + g if s < 2 else s - 1 + g
+                    else:
+                        turn = s
                     v_plan.setdefault(turn, []).append((s, g))
 
         def open_degrees(s):
@@ -383,8 +386,8 @@ def tile_allgnn_pa_kernel(tc, x, adj, W_in, b_in, out):
                 transposes(s1, 1)
             if sp >= 0 and s1 < NS - 1:
                 finish(sp)
-            if s1 + ABUFS < NS:
-                load_adj(s1 + ABUFS)
+            if 0 <= s0 and s0 + ABUFS < NS:
+                load_adj(s0 + ABUFS)
             if more:
                 quantise(s1, 0, 512)
             if s0 >= 0:

@@ -25,7 +25,7 @@ NPASS = NODES // 512
 ROWW = NODES // 2
 BANKS = 3 * G
 ABUFS = 8
-DEGN = 26
+DEGN = 4
 FOLD = 256
 PIN = True
 MODES = ["PP", "VV"] * 6
@@ -203,7 +203,7 @@ def tile_allgnn_pa_kernel(tc, x, adj, W_in, b_in, out):
             for g in range(G):
                 if MODES[s][g] == "V":
                     if MODES[s] == "VV":
-                        turn = s + g if s < 2 else s - 1 + g
+                        turn = s + g if s < 4 else s - 1 + g
                     else:
                         turn = s
                     v_plan.setdefault(turn, []).append((s, g))

@@ -25,7 +25,7 @@ NPASS = NODES // 512
 ROWW = NODES // 2
 BANKS = 3 * G
 ABUFS = 8
-DEGN = 4
+DEGN = 26
 FOLD = 256
 PIN = True
 MODES = ["PP", "VV"] * 6
@@ -209,10 +209,13 @@ def tile_allgnn_pa_kernel(tc, x, adj, W_in, b_in, out):
                     v_plan.setdefault(turn, []).append((s, g))
 
         def open_degrees(s):
+            if s in dp1_tiles:
+                return
             dp1 = small.tile([P, G], F32, name="dp1")
             dp1_tiles[s] = dp1
 
         def vector_degrees(s, g):
+            open_degrees(s)
             nc.vector.tensor_scalar(
                 out=junk[:],
                 in0=a_tiles[s][:, g * NODES : (g + 1) * NODES],
@@ -246,7 +249,10 @@ def tile_allgnn_pa_kernel(tc, x, adj, W_in, b_in, out):
 
         def open_acc(s):
             acc = ps_a.tile([P, 4, HID], F32, name="acc")
-            acc_tiles[s] = acc
+            acc_tiles[s] = [acc[:, g, :] for g in range(G)]
+            if s == NS - 1:
+                own = ps_t.tile([P, 2, 2, P], F32, name="tp")
+                acc_tiles[s][G - 1] = own[:, 0, 0, :]
 
         def aggregate(s):
             acc = acc_tiles[s]
@@ -254,7 +260,7 @@ def tile_allgnn_pa_kernel(tc, x, adj, W_in, b_in, out):
                 for c in range(NPASS):
                     cols = slice(g * 768 + c * P, g * 768 + (c + 1) * P)
                     nc.tensor.matmul_mx(
-                        out=acc[:, g, :],
+                        out=acc[g],
                         lhsT=c_tiles[s][:, cols].bitcast(FP8X4),
                         lhsT_scale=s_tiles[s][:, cols],
                         rhs=h_codes[:, c * HID : (c + 1) * HID].bitcast(FP8X4),
@@ -330,7 +336,7 @@ def tile_allgnn_pa_kernel(tc, x, adj, W_in, b_in, out):
             for g in range(G):
                 nc.scalar.activation(
                     out=o_sb[:, g * HID : (g + 1) * HID],
-                    in_=acc_tiles[s][:, g, :],
+                    in_=acc_tiles[s][g],
                     func=ACTF.Copy,
                     scale=rec_tiles[s][:, g : g + 1],
                 )
@@ -367,8 +373,8 @@ def tile_allgnn_pa_kernel(tc, x, adj, W_in, b_in, out):
             if more and s0 >= 0:
                 quantise(s0, 1024, 1536)
             if s0 == NS - 1:
-                quantise(s0, 1024, 1280)
                 reciprocals(s0)
+                quantise(s0, 1024, 1280)
             if sp >= 0:
                 reciprocals(sp)
             if s0 == NS - 1:

@@ -350,14 +350,14 @@ def tile_allgnn_pa_kernel(tc, x, adj, W_in, b_in, out):
         for c in range(NPASS + 3):
             if c < NPASS:
                 stage1_transpose(c)
-                if c == 0:
-                    spread_bias()
             elif c < NPASS + G:
                 transposes(0, c - NPASS)
             if 0 <= c - 1 < NPASS:
                 stage1_quantise(c - 1)
             if c == 1:
                 weights()
+            if c == 2:
+                spread_bias()
             if 0 <= c - 2 < NPASS:
                 ps1_tiles[c - 2] = stage1_matmul(c - 2)
                 stage1_bias(c - 2, ps1_tiles[c - 2])

from contextlib import ExitStack

import concourse.mybir as mybir
from concourse.masks import make_identity

F32 = mybir.dt.float32
BF16 = mybir.dt.bfloat16
U32 = mybir.dt.uint32
U8 = mybir.dt.uint8
I32 = mybir.dt.int32
FP8X4 = mybir.dt.float8_e4m3fn_x4
ALU = mybir.AluOpType
ACTF = mybir.ActivationFunctionType
AX = mybir.AxisListType

P = 128
NODES = 3072
FEAT = 512
HID = 128
FLOPS = 2 * NODES * FEAT * HID + 2 * NODES * NODES * HID

G = 2
NS = NODES // (P * G)
NPASS = NODES // 512
ROWW = NODES // 2
BANKS = 3 * G
ABUFS = 8
DEGN = 26
FOLD = 256
PIN = True
MODES = ["PP", "VV"] * 6
HALVES = 4


def tile_allgnn_pa_kernel(tc, x, adj, W_in, b_in, out):
    nc = tc.nc
    adj_v = adj.rearrange("(s p g) j -> s p (g j)", p=P, g=G)
    out_v = out.rearrange("(s p g) h -> s p (g h)", p=P, g=G)
    x_v = x.rearrange("(c u p e) k -> c p u (e k)", c=NPASS, u=2, p=P, e=2)
    w_v = W_in.rearrange("(u p e) h -> p u (e h)", u=2, p=P, e=2)

    with ExitStack() as ctx:
        const = ctx.enter_context(tc.tile_pool(name="const", bufs=1))
        apool = ctx.enter_context(tc.tile_pool(name="apool", bufs=ABUFS))
        gpool = ctx.enter_context(tc.tile_pool(name="gpool", bufs=3))
        small = ctx.enter_context(tc.tile_pool(name="small", bufs=5))
        ps_t = ctx.enter_context(tc.psum_pool(name="ps_t", bufs=5))
        ps_a = ctx.enter_context(tc.psum_pool(name="ps_a", bufs=2))
        ps_d = ctx.enter_context(tc.psum_pool(name="ps_d", bufs=1))
        if PIN:
            ctx.enter_context(tc.manual_schedule())

        w_raw = const.tile([P, 4 * HID], BF16)
        b_row = const.tile([P, HID], BF16)
        nc.vector.memset(b_row[:].bitcast(I32), 0)
        nc.scalar.dma_start(out=b_row[0:1, :], in_=b_in.unsqueeze(0))
        x_sb = const.tile([P, NPASS * 2048], BF16)
        for u in range(2):
            nc.sync.dma_start(out=x_sb[:, u * 1024 : (u + 1) * 1024], in_=x_v[0][:, u, :])
        for c in range(1, NPASS):
            nc.sync.dma_start(
                out=x_sb[:, c * 2048 : (c + 1) * 2048].rearrange("p (u f) -> p u f", u=2),
                in_=x_v[c],
            )
            if c == 1:
                nc.sync.dma_start(out=w_raw[:].rearrange("p (u f) -> p u f", u=2), in_=w_v)
        a_tiles = {}

        def load_adj(s):
            a_sb = apool.tile([P, G * NODES], BF16, name="a_sb")
            n_piece = G if s < HALVES else 1
            width = G * NODES // n_piece
            for i in range(n_piece):
                nc.sync.dma_start(
                    out=a_sb[:, i * width : (i + 1) * width], in_=adj_v[s][:, i * width : (i + 1) * width]
                )
            a_tiles[s] = a_sb

        for s in range(ABUFS):
            load_adj(s)

        ident = const.tile([P, P], F32)
        make_identity(nc, ident[:])
        ones = const.tile([P, P], BF16)
        nc.vector.memset(ones[:], 1.0)
        fold_q = const.tile([P, 32], F32)
        nc.vector.tensor_reduce(
            out=fold_q[:], in_=ident[:].rearrange("p (q t) -> p q t", t=4), axis=AX.X, op=ALU.add
        )
        fold = const.tile([P, 4, 32], F32)
        nc.vector.tensor_copy(out=fold[:], in_=fold_q[:].unsqueeze(1).to_broadcast([P, 4, 32]))
        quad = const.tile([P, 4], F32)
        nc.vector.tensor_reduce(
            out=quad[:], in_=ident[:].rearrange("p (r q) -> p r q", q=32), axis=AX.X, op=ALU.add
        )
        junk = const.tile([P, NODES], BF16)

        w_grp = const.tile([P, 4 * HID], BF16, align_bytes=64)
        w_codes = const.tile([P, HID], U32, align_bytes=64)
        w_scales = const.tile([P, HID], U8, align_bytes=64)

        def weights():
            nc.vector.tensor_copy(
                out=w_grp[:].rearrange("p (h t) -> p h t", t=4),
                in_=w_raw[:].rearrange("p (t h) -> p h t", t=4),
            )
            nc.vector.quantize_mx(out=w_codes[:].bitcast(FP8X4), scales=w_scales[:], in_=w_grp[:])

        x_codes = const.tile([P, NPASS * 512], U32, align_bytes=64)
        x_scales = const.tile([P, NPASS * 512], U8, align_bytes=64)
        h_grp = const.tile([P, NPASS * 512], BF16, align_bytes=64)
        h_codes = const.tile([P, NPASS * HID], U32, align_bytes=64)
        h_scales = const.tile([P, NPASS * HID], U8, align_bytes=64)

        def transpose_bank(words, offs):
            tp = ps_t.tile([P, 2, 2, P], F32, name="tp")
            for n in range(2):
                for u in range(2):
                    o = offs[n] + P * u
                    nc.tensor.transpose(tp[:, n, u, :], words[:, o : o + P], ident[:])
            return tp

        def copy_bank(tp, dst_words):
            nc.scalar.copy(
                out=dst_words.rearrange("p (n i u) -> p n i u", n=2, i=P, u=2),
                in_=tp[:].rearrange("p n u i -> p n i u"),
            )

        bias = const.tile([P, HID], BF16)

        def spread_bias():
            bb = ps_d.tile([P, 512], F32, name="de")
            nc.tensor.matmul(out=bb[:, 0:HID], lhsT=ones[:], rhs=b_row[:], start=True, stop=True)
            nc.vector.tensor_copy(out=bias[:], in_=bb[:, 0:HID])

        x_words = x_sb[:].bitcast(F32)
        gx_tiles = {}

        def stage1_transpose(c):
            gx = gpool.tile([P, 2048], BF16, name="gx", align_bytes=64)
            gx_tiles[c] = gx
            gxw = gx[:].bitcast(F32)
            for k in range(2):
                tp = transpose_bank(x_words, [(c * 4 + 2 * k + n) * 256 for n in range(2)])
                copy_bank(tp, gxw[:, k * 512 : (k + 1) * 512])

        def stage1_quantise(c):
            nc.vector.quantize_mx(
                out=x_codes[:, c * 512 : (c + 1) * 512].bitcast(FP8X4),
                scales=x_scales[:, c * 512 : (c + 1) * 512],
                in_=gx_tiles[c][:],
            )

        def stage1_matmul(c):
            ps1 = ps_a.tile([P, 4, HID], F32, name="acc")
            for t in range(4):
                cols = slice(c * 512 + t * P, c * 512 + (t + 1) * P)
                nc.tensor.matmul_mx(
                    out=ps1[:, t, :],
                    lhsT=x_codes[:, cols].bitcast(FP8X4),
                    lhsT_scale=x_scales[:, cols],
                    rhs=w_codes[:].bitcast(FP8X4),
                    rhs_scale=w_scales[:],
                    start=True,
                    stop=True,
                )
            return ps1

        def stage1_bias(c, ps1):
            hs = slice(c * 512, (c + 1) * 512)
            nc.vector.tensor_tensor(
                out=h_grp[:, hs].rearrange("p (h t) -> p h t", t=4),
                in0=ps1[:].rearrange("p t h -> p h t"),
                in1=bias[:].unsqueeze(2).to_broadcast([P, HID, 4]),
                op=ALU.add,
            )

        def stage1_quantise_h(c):
            hs = slice(c * 512, (c + 1) * 512)
            nc.vector.quantize_mx(
                out=h_codes[:, c * HID : (c + 1) * HID].bitcast(FP8X4),
                scales=h_scales[:, c * HID : (c + 1) * HID],
                in_=h_grp[:, hs],
            )

        g_tiles = {}
        c_tiles = {}
        s_tiles = {}
        acc_tiles = {}
        de_tiles = {}
        dsb_tiles = {}
        dp1_tiles = {}
        rec_tiles = {}
        pick_tiles = {}

        def p_list(s):
            if s < 0:
                return []
            return [g for g in range(G) if MODES[s][g] == "P"]

        v_plan = {}
        for s in range(NS):
            for g in range(G):
                if MODES[s][g] == "V":
                    if MODES[s] == "VV":
                        turn = s + g if s < 4 else s - 1 + g
                    else:
                        turn = s
                    v_plan.setdefault(turn, []).append((s, g))

        def open_degrees(s):
            if s in dp1_tiles:
                return
            dp1 = small.tile([P, G], F32, name="dp1")
            dp1_tiles[s] = dp1

        def vector_degrees(s, g):
            open_degrees(s)
            nc.vector.tensor_scalar(
                out=junk[:],
                in0=a_tiles[s][:, g * NODES : (g + 1) * NODES],
                scalar1=1.0,
                scalar2=1.0,
                op0=ALU.mult,
                op1=ALU.add,
                accum_out=dp1_tiles[s][:, g : g + 1],
            )

        def transposes(s, g):
            if g == 0:
                grp = gpool.tile([P, G * NODES], BF16, name="grp", align_bytes=64)
                codes = gpool.tile([P, G * 768], U32, name="codes", align_bytes=64)
                scales = gpool.tile([P, G * 768], U8, name="scales", align_bytes=64)
                g_tiles[s] = grp
                c_tiles[s] = codes
                s_tiles[s] = scales
            gw = g_tiles[s][:].bitcast(F32)
            aw = a_tiles[s][:].bitcast(F32)
            for kk in range(3):
                tp = transpose_bank(aw, [g * ROWW + (2 * kk + n) * 256 for n in range(2)])
                copy_bank(tp, gw[:, g * ROWW + kk * 512 : g * ROWW + (kk + 1) * 512])

        def quantise(s, w0, w1):
            nc.vector.quantize_mx(
                out=c_tiles[s][:, w0:w1].bitcast(FP8X4),
                scales=s_tiles[s][:, w0:w1],
                in_=g_tiles[s][:, 4 * w0 : 4 * w1],
            )

        def open_acc(s):
            acc = ps_a.tile([P, 4, HID], F32, name="acc")
            acc_tiles[s] = [acc[:, g, :] for g in range(G)]
            if s == NS - 1:
                own = ps_t.tile([P, 2, 2, P], F32, name="tp")
                acc_tiles[s][G - 1] = own[:, 0, 0, :]

        def aggregate(s):
            acc = acc_tiles[s]
            for g in range(G):
                for c in range(NPASS):
                    cols = slice(g * 768 + c * P, g * 768 + (c + 1) * P)
                    nc.tensor.matmul_mx(
                        out=acc[g],
                        lhsT=c_tiles[s][:, cols].bitcast(FP8X4),
                        lhsT_scale=s_tiles[s][:, cols],
                        rhs=h_codes[:, c * HID : (c + 1) * HID].bitcast(FP8X4),
                        rhs_scale=h_scales[:, c * HID : (c + 1) * HID],
                        start=(c == 0),
                        stop=(c == NPASS - 1),
                    )

        def tensor_degrees(s):
            de = ps_d.tile([P, 512], F32, name="de")
            de_tiles[s] = de
            for n, g in enumerate(p_list(s)):
                for r in range(4):
                    col = (n * 4 + r) * DEGN
                    for c in range(NPASS):
                        o = g * NODES + c * 512 + r * P
                        nc.tensor.matmul(
                            out=de[:, col : col + DEGN],
                            lhsT=g_tiles[s][:, o : o + P],
                            rhs=ones[:, 0:DEGN],
                            start=(c == 0),
                            stop=(c == NPASS - 1),
                        )

        def degrees_to_sbuf(s):
            npt = len(p_list(s))
            dsb = small.tile([P, 4 * G], F32, name="dsb")
            dsb_tiles[s] = dsb
            nc.scalar.activation(
                out=dsb[:, 0 : 4 * npt].unsqueeze(2),
                in_=de_tiles[s][:, 0 : 4 * npt * DEGN].rearrange("p (r n) -> p r n", n=DEGN)[:, :, 0:1],
                func=ACTF.Copy,
                bias=0.25,
            )

        def fold_degrees(s):
            w = 4 * len(p_list(s))
            nc.tensor.matmul(
                out=de_tiles[s][:, FOLD : FOLD + w],
                lhsT=fold[:].rearrange("p r q -> p (r q)"),
                rhs=dsb_tiles[s][:, 0:w],
                start=True,
                stop=True,
            )

        def pick_degrees(s):
            w = 4 * len(p_list(s))
            pick = small.tile([P, 4 * G], F32, name="pick")
            pick_tiles[s] = pick
            nc.vector.tensor_tensor(
                out=pick[:, 0:w].rearrange("p (n r) -> p n r", r=4),
                in0=de_tiles[s][:, FOLD : FOLD + w].rearrange("p (n r) -> p n r", r=4),
                in1=quad[:].unsqueeze(1).to_broadcast([P, w // 4, 4]),
                op=ALU.mult,
            )

        def sum_picked(s):
            gs = p_list(s)
            nc.vector.tensor_reduce(
                out=dp1_tiles[s][:, gs[0] : gs[-1] + 1],
                in_=pick_tiles[s][:, 0 : 4 * len(gs)].rearrange("p (n r) -> p n r", r=4),
                axis=AX.X,
                op=ALU.add,
            )

        def reciprocals(s):
            rec = small.tile([P, G], F32, name="rec")
            rec_tiles[s] = rec
            nc.vector.reciprocal(out=rec[:], in_=dp1_tiles[s][:])

        def finish(s):
            o_sb = small.tile([P, G * HID], F32, name="o_sb")
            for g in range(G):
                nc.scalar.activation(
                    out=o_sb[:, g * HID : (g + 1) * HID],
                    in_=acc_tiles[s][g],
                    func=ACTF.Copy,
                    scale=rec_tiles[s][:, g : g + 1],
                )
                if s == NS - 1:
                    cols = slice(g * HID, (g + 1) * HID)
                    nc.sync.dma_start(out=out_v[s][:, cols], in_=o_sb[:, cols])
            if s < NS - 1:
                nc.sync.dma_start(out=out_v[s], in_=o_sb[:])

        ps1_tiles = {}
        for c in range(NPASS + 3):
            if c < NPASS:
                stage1_transpose(c)
            elif c < NPASS + G:
                transposes(0, c - NPASS)
            if 0 <= c - 1 < NPASS:
                stage1_quantise(c - 1)
            if c == 1:
                weights()
            if c == 2:
                spread_bias()
            if 0 <= c - 2 < NPASS:
                ps1_tiles[c - 2] = stage1_matmul(c - 2)
                stage1_bias(c - 2, ps1_tiles[c - 2])
            if 0 <= c - 3 < NPASS:
                stage1_quantise_h(c - 3)

        open_degrees(0)
        for tau in range(-1, NS):
            sp, s0, s1 = tau - 1, tau, tau + 1
            more = s1 < NS
            if more and s0 >= 0:
                transposes(s1, 0)
            if more and s0 >= 0:
                quantise(s0, 1024, 1536)
            if s0 == NS - 1:
                reciprocals(s0)
                quantise(s0, 1024, 1280)
            if sp >= 0:
                reciprocals(sp)
            if s0 == NS - 1:
                quantise(s0, 1280, 1536)
            if p_list(s0):
                tensor_degrees(s0)
                degrees_to_sbuf(s0)
            if s1 + 1 < NS:
                open_degrees(s1 + 1)
            for s, g in v_plan.get(s1, []):
                vector_degrees(s, g)
            if sp >= 0 and s1 >= NS - 1:
                finish(sp)
            if more and s0 >= 0:
                transposes(s1, 1)
            if sp >= 0 and s1 < NS - 1:
                finish(sp)
            if 0 <= s0 and s0 + ABUFS < NS:
                load_adj(s0 + ABUFS)
            if more:
                quantise(s1, 0, 512)
            if s0 >= 0:
                open_acc(s0)
            if p_list(s0):
                fold_degrees(s0)
            if s0 >= 0:
                aggregate(s0)
            if p_list(s0):
                pick_degrees(s0)
            if more:
                quantise(s1, 512, 1024)
            if p_list(s0):
                sum_picked(s0)
        finish(NS - 1)
